import numpy as np
import ml_dtypes


def mxq(x, axis, fmt="e4m3"):
    dtype, down = {"e4m3": (ml_dtypes.float8_e4m3fn, 7), "e5m2": (ml_dtypes.float8_e5m2, 14)}[fmt]
    v = np.moveaxis(np.asarray(x, np.float32).astype(ml_dtypes.bfloat16).astype(np.float64), axis, -1)
    blocks = v.reshape(v.shape[:-1] + (-1, 32))
    amax = np.abs(blocks).max(-1, keepdims=True)
    byte = np.maximum(np.where(amax > 0, np.frexp(amax)[1] - 1 + 127, 0) - down, 1)
    scale = np.exp2(byte - 127.0)
    codes = (blocks / scale).astype(np.float32).astype(dtype).astype(np.float64)
    return np.moveaxis((codes * scale).reshape(v.shape), -1, axis)


WIDE = False


def mx_kscale(k):
    if not WIDE:
        return np.ones(k)
    levels = np.array([10, -10, 5, -5, 0])
    if k % 512:
        return np.exp2(np.random.permutation(np.resize(levels, k // 32))).repeat(32)
    a = np.empty((k // 512, 16))
    for p in range(k // 512):
        a[p, :8] = np.random.permutation(np.resize(levels, 8))
        for g in range(8):
            far = levels[np.abs(levels - a[p, g]) >= 10]
            a[p, g + 8] = far[np.random.randint(len(far))]
    return np.exp2(a.ravel()).repeat(32)


BF16 = ml_dtypes.bfloat16


def bf(x):
    return np.asarray(x, np.float32).astype(BF16)


def f64(x):
    return np.asarray(x).astype(np.float64)


B, D_IN, D_HID, D_OUT = 1024, 512, 4096, 512
EPS = 1e-12
NORM_MAX = 16


def draw0():
    s, t = mx_kscale(D_IN), mx_kscale(D_HID)
    return {
        "x": bf(np.random.standard_normal((B, D_IN))),
        "in_mean": bf(np.random.standard_normal(D_IN) * 0.1),
        "in_std": bf(np.random.uniform(0.5, 1.5, D_IN) / s),
        "out_mean": bf(np.random.standard_normal(D_OUT) * 0.1),
        "out_std": bf(np.random.uniform(0.5, 1.5, D_OUT)),
        "W1": bf(np.random.standard_normal((D_HID, D_IN)) / np.sqrt(D_IN) / s[None, :] * t[:, None]),
        "b1": bf(np.random.standard_normal(D_HID) * 0.1 * t),
        "W2": bf(np.random.standard_normal((D_OUT, D_HID)) * 0.85 / np.sqrt(D_HID) / t[None, :]),
        "b2": bf(np.random.standard_normal(D_OUT) * 0.1),
        "norm_max": NORM_MAX,
    }


def core(x, in_mean, in_std, out_mean, out_std, W1, b1, W2, b2, norm_max):
    x, in_mean, in_std, out_mean, out_std = f64(x), f64(in_mean), f64(in_std), f64(out_mean), f64(out_std)
    norm_max = float(norm_max)
    x_copy = x[..., :D_OUT]
    xn = (x - in_mean) / in_std
    h = np.maximum((mxq(xn, 1, "e4m3") @ mxq(f64(W1), 1, "e4m3").T) + f64(b1), 0.0)
    res = (mxq(h, 1, "e4m3") @ mxq(f64(W2), 1, "e4m3").T) + f64(b2)
    norms = np.sqrt((res * res).sum(-1, keepdims=True))
    scale = norm_max / norms
    res = np.where(norms > norm_max, res * scale, res)
    res = res * out_std + out_mean - in_mean
    mapped = res + x_copy
    mnorm = np.sqrt((mapped * mapped).sum(-1, keepdims=True))
    return mapped / np.maximum(mnorm, EPS)


def e4m3fn_bytes(y):
    return np.clip(np.asarray(y, np.float64), -448.0, 448.0).astype(np.float32).astype(ml_dtypes.float8_e4m3fn).view(np.uint8)


def e4m3fn_values(b):
    return np.asarray(b, np.uint8).view(ml_dtypes.float8_e4m3fn).astype(np.float64)


def setup_inputs():
    d = draw0()
    x0 = np.asarray(d['W2']).astype(np.float64)
    s = (np.max(np.abs(x0), axis=(0,), keepdims=True) / 448.0).astype(np.float32)
    out = {}
    for k, v in d.items():
        if k == 'W2':
            out['W2_bytes'] = e4m3fn_bytes(x0 / s.astype(np.float64))
            out['W2_scale'] = s
        else:
            out[k] = v
    return out


def reference(x, in_mean, in_std, out_mean, out_std, W1, b1, W2_bytes, W2_scale, b2, norm_max):
    return core(x, in_mean, in_std, out_mean, out_std, W1, b1, e4m3fn_values(W2_bytes) * W2_scale.astype(np.float64), b2, norm_max)

@@ -1,0 +1,424 @@
+from contextlib import ExitStack
+
+import concourse.mybir as mybir
+from concourse.masks import make_identity
+
+B, D_IN, D_HID, D_OUT = 1024, 512, 4096, 512
+FLOPS = 2 * B * D_IN * D_HID + 2 * B * D_HID * D_OUT
+
+F32 = mybir.dt.float32
+BF16 = mybir.dt.bfloat16
+U32 = mybir.dt.uint32
+U8 = mybir.dt.uint8
+FP8 = mybir.dt.float8_e4m3fn
+FP8X4 = mybir.dt.float8_e4m3fn_x4
+OP = mybir.AluOpType
+ACT = mybir.ActivationFunctionType
+
+P = 128
+W2STEPS = [0, 1, 2, 3, 5, 6, 8, 9]
+XB = 2
+XBV = 0
+PSTEPS = [0, 2, 4, 7]
+EP = {12: 'aR2 aR1 aR3 aQ1 aF2 aR0', 14: 'aF1 aQ0 aF3 aF0 aM0 aM1 aN0 aQ2', 15: 'aQ3 aM2', 16: 'aO0 aM3 aN1 aN3', 17: 'bR0 bR1 bF1 aO3 bF0 aN2', 18: 'aO1 bQ1 aO2 bQ0', 19: 'bM0 bM1', 20: 'bN0 bR2 bN1 bR3 bO0 bO1 bQ2 bF2 bM2 bQ3 bF3 bN2 bM3 bN3 bO2 bO3'}
+VOUT = ['bO2', 'bO3', 'aO3', 'bO1', 'aO0', 'bO0']
+BP = {14: '00 10 02 20 01 30 11 21', 15: '12 22 03 13 23 31 33 41', 16: '32 51 40 61', 17: '50 60 70 71', 19: '43 52 53', 18: '42'}
+LOADS = 'x0 w0 c0 w2 w1 c1 w5 c3 w7 w3 x1 w4 c2 w6'
+GROUPS = 8
+HALF = 512
+TILES = 4
+
+
+def tile_mlp_kernel(
+    tc, x, in_mean, in_std, out_mean, out_std, W1, b1, W2_bytes, W2_scale, b2, norm_max, out
+):
+    nc = tc.nc
+    inv_nm2 = 1.0 / (float(norm_max) * float(norm_max))
+
+    with ExitStack() as ctx:
+        keep = ctx.enter_context(tc.tile_pool(name="keep", bufs=1))
+        pool = ctx.enter_context(tc.tile_pool(name="work", bufs=2))
+        psum = ctx.enter_context(tc.psum_pool(name="psum", bufs=1))
+        ctx.enter_context(tc.manual_schedule(engines={mybir.EngineType.PE, mybir.EngineType.SP}))
+
+        def kept(name, shape, dtype):
+            return keep.tile(shape, dtype, name=name, align_bytes=64)
+
+        def work(tag, shape, dtype, bufs):
+            return pool.tile(shape, dtype, name=tag, tag=tag, bufs=bufs, align_bytes=64)
+
+        ring_next = [0]
+
+        def ring():
+            tag = "ring%d" % (ring_next[0] % 4)
+            ring_next[0] += 1
+            return psum.tile([P, 512], F32, name=tag, tag=tag)
+
+        mean_col = kept("mean_col", [P, 4], BF16)
+        std_col = kept("std_col", [P, 4], BF16)
+        vecs = kept("vecs", [P, 512], BF16)
+        x_sb = {}
+        for half in range(2):
+            for pair in range(2):
+                x_sb[half, pair] = kept("x_sb%d%d" % (half, pair), [P, 2, D_IN], BF16)
+        w1_sb = [kept("w1_sb%d" % g, [P, 4, D_IN], BF16) for g in range(GROUPS)]
+        sc_sb = [kept("sc_sb%d" % c, [P, 1024], F32) for c in range(4)]
+        w2_bytes_sb = [kept("w2_bytes_sb%d" % c, [P, 4, 1024], U8) for c in range(4)]
+        b2_bc = kept("b2_bc", [P, D_OUT], BF16)
+        ostd_bc = kept("ostd_bc", [P, D_OUT], BF16)
+
+        def load_x(half):
+            rows = x[half * HALF : (half + 1) * HALF, :].rearrange("(p i) k -> p i k", i=4)
+            for pair in range(2):
+                nc.sync.dma_start(out=x_sb[half, pair][:], in_=rows[:, 2 * pair : 2 * pair + 2, :])
+
+        def load_w1(g):
+            rows = W1[512 * g : 512 * (g + 1), :].rearrange("(m t) k -> m t k", t=4)
+            nc.sync.dma_start(out=w1_sb[g][:], in_=rows)
+
+        def load_w2(c):
+            cols = slice(1024 * c, 1024 * (c + 1))
+            nc.sync.dma_start(
+                out=sc_sb[c][:], in_=W2_scale[:, cols].rearrange("o k -> (o k)").partition_broadcast(P)
+            )
+            nc.sync.dma_start(
+                out=w2_bytes_sb[c][:], in_=W2_bytes[:, cols].rearrange("(j p) k -> p j k", p=P)
+            )
+
+        nc.vector.memset(vecs[:], 0.0)
+        warm = kept("warm", [P, 1], F32)
+        nc.vector.memset(warm[:], 0.0)
+        nc.scalar.dma_start(out=mean_col[:], in_=in_mean.rearrange("(p t) -> p t", t=4))
+        nc.scalar.dma_start(out=std_col[:], in_=in_std.rearrange("(p t) -> p t", t=4))
+        nc.scalar.dma_start(out=vecs[0:8, :], in_=b1.rearrange("(g k) -> g k", g=GROUPS))
+        nc.scalar.dma_start(out=vecs[8:9, :], in_=out_mean.rearrange("(o k) -> o k", o=1))
+        nc.scalar.dma_start(out=vecs[9:10, :], in_=in_mean.rearrange("(o k) -> o k", o=1))
+        for item in LOADS.split():
+            {"x": load_x, "w": load_w1, "c": load_w2}[item[0]](int(item[1]))
+        nc.sync.dma_start(out=b2_bc[:], in_=b2.partition_broadcast(P))
+        nc.sync.dma_start(out=ostd_bc[:], in_=out_std.partition_broadcast(P))
+
+        ident_f = kept("ident_f", [P, P], F32)
+        make_identity(nc, ident_f[:])
+        ident_b = kept("ident_b", [P, P], BF16)
+        make_identity(nc, ident_b[:])
+        neg_half = kept("neg_half", [P, 1], F32)
+        nc.gpsimd.memset(neg_half[:], -0.5)
+
+        nc.scalar.activation(out=warm[:], in_=warm[:], func=ACT.Relu)
+
+        def codes(name):
+            return kept(name + "_codes", [P, 512], U32), kept(name + "_scales", [P, 512], U8)
+
+        xc = [codes("xc%d" % h) for h in range(2)]
+        w1c = [codes("w1c%d" % g) for g in range(GROUPS)]
+        w2c = [codes("w2c%d" % g) for g in range(GROUPS)]
+        hc = [codes("hc%d" % g) for g in range(GROUPS)]
+
+        def quantize(dst, src, cols=slice(0, 512)):
+            nc.vector.quantize_mx(
+                out=dst[0][:, cols].bitcast(FP8X4),
+                scales=dst[1][:, cols],
+                in_=src[:].rearrange("p n t -> p (n t)"),
+            )
+
+
+        rstd = kept("rstd", [P, 4], F32)
+        mean_f = kept("mean_f", [P, 4], F32)
+        nmr = kept("nmr", [P, 4], F32)
+        nc.vector.reciprocal(out=rstd[:], in_=std_col[:])
+        nc.vector.tensor_copy(out=mean_f[:], in_=mean_col[:])
+        nc.vector.scalar_tensor_tensor(
+            out=nmr[:], in0=mean_col[:], scalar=-1.0, in1=rstd[:], op0=OP.mult, op1=OP.mult
+        )
+
+        def x_path(half, vector_u):
+            planes = work("planes", [P, 4, 512], BF16, 3)
+            inter = work("inter", [P, 512, 4], BF16, 3)
+            for pair in range(2):
+                bank = ring()
+                words = x_sb[half, pair][:].bitcast(F32)
+                for u in range(2):
+                    for i in range(2):
+                        col = 256 * u + 128 * i
+                        nc.tensor.transpose(bank[:, col : col + 128], words[:, i, u:256:2], ident_f[:])
+                toks = slice(256 * pair, 256 * pair + 256)
+                for t in range(4):
+                    u, e = t // 2, t % 2
+                    src = bank[:, 256 * u : 256 * u + 256].bitcast(BF16).rearrange("p (n e) -> p e n", e=2)[:, e, :]
+                    if pair < vector_u:
+                        nc.vector.tensor_scalar(
+                            out=planes[:, t, toks], in0=src, scalar1=mean_f[:, t : t + 1],
+                            scalar2=rstd[:, t : t + 1], op0=OP.subtract, op1=OP.mult,
+                        )
+                    else:
+                        nc.scalar.activation(
+                            out=planes[:, t, toks], in_=src, func=ACT.Identity,
+                            scale=rstd[:, t : t + 1], bias=nmr[:, t : t + 1],
+                        )
+            for pair in range(2):
+                toks = slice(256 * pair, 256 * pair + 256)
+                nc.vector.tensor_copy(
+                    out=inter[:, toks, :].rearrange("p (c i) t -> p c t i", i=4),
+                    in_=planes[:, :, toks].rearrange("p t (c i) -> p c t i", i=4),
+                )
+            return inter
+
+        w1g = {}
+        w2s = {}
+        w2g = {}
+
+        def transposes(words4, first):
+            bank = ring()
+            for s in range(2):
+                for u in range(2):
+                    col = 256 * s + 128 * u
+                    nc.tensor.transpose(bank[:, col : col + 128], words4[:, first + s, u:256:2], ident_f[:])
+            return bank
+
+        def copy_out(dst, bank, first):
+            nc.scalar.copy(
+                out=dst[:].bitcast(F32)[:, 128 * first : 128 * first + 256, :].rearrange(
+                    "p (s m) u -> p s m u", s=2
+                ),
+                in_=bank[:].rearrange("p (s u m) -> p s m u", s=2, u=2),
+            )
+
+        def prep_w1(g):
+            w1g[g] = work("w1g", [P, 512, 4], BF16, 2)
+            for first in (0, 2):
+                bank = transposes(w1_sb[g][:].bitcast(F32), first)
+                copy_out(w1g[g], bank, first)
+
+        def scale_w2(c):
+            w2s[c] = work("w2s", [P, 4, 1024], BF16, 2)
+            for j in range(4):
+                nc.vector.tensor_tensor(
+                    out=w2s[c][:, j, :], in0=w2_bytes_sb[c][:, j, :].bitcast(FP8), in1=sc_sb[c][:], op=OP.mult
+                )
+
+        def prep_w2(g):
+            w2g[g] = work("w2g", [P, 512, 4], BF16, 2)
+            for first in (0, 2):
+                bank = transposes(w2s[g // 2][:].bitcast(F32)[:, :, 256 * (g % 2) : 256 * (g % 2) + 256], first)
+                copy_out(w2g[g], bank, first)
+
+        b1_f = kept("b1_f", [P, 32], F32)
+
+        def bias_columns():
+            bank = ring()
+            words = vecs[:].bitcast(F32)
+            for u in range(2):
+                nc.tensor.transpose(bank[:, 128 * u : 128 * u + 128], words[:, u:256:2], ident_f[:])
+            b1_w = kept("b1_w", [P, 8, 2], F32)
+            nc.vector.tensor_copy(
+                out=b1_w[:], in_=bank[:, 0:256].rearrange("p (u g) -> p g u", u=2)[:, 0:8, :]
+            )
+            nc.vector.tensor_copy(out=b1_f[:], in_=b1_w[:].rearrange("p g u -> p (g u)").bitcast(BF16))
+
+        h_planes = {}
+        h_inter = {}
+
+        def matmul1(half, g, t, bank, cols, n0, n):
+            lanes = slice(128 * t, 128 * t + 128)
+            nc.tensor.matmul_mx(
+                out=bank[:, cols],
+                lhsT=w1c[g][0][:, lanes].bitcast(FP8X4), lhsT_scale=w1c[g][1][:, lanes],
+                rhs=xc[half][0][:, n0 : n0 + n].bitcast(FP8X4), rhs_scale=xc[half][1][:, n0 : n0 + n],
+                start=True, stop=True,
+            )
+
+        def relu(planes, t, g, bank, cols):
+            nc.scalar.activation(
+                out=planes[:, t, :], in_=bank[:, cols], func=ACT.Relu, bias=b1_f[:, 4 * g + t : 4 * g + t + 1]
+            )
+
+        def stage1(half, g, between):
+            planes = work("planes", [P, 4, 512], BF16, 3)
+            h_planes[g] = planes
+            for t in range(4):
+                bank = ring()
+                matmul1(half, g, t, bank, slice(0, 512), 0, 512)
+                relu(planes, t, g, bank, slice(0, 512))
+                if t == 1:
+                    between()
+
+        def stage1_quarter(half, g, part, between):
+            planes = work("planes", [P, 4, 512], BF16, 3)
+            h_planes[g] = planes
+            for pair in range(2):
+                bank = ring()
+                for s in range(2):
+                    matmul1(half, g, 2 * pair + s, bank, slice(256 * s, 256 * s + 256), 256 * part, 256)
+                for s in range(2):
+                    nc.scalar.activation(
+                        out=planes[:, 2 * pair + s, 0:256], in_=bank[:, 256 * s : 256 * s + 256], func=ACT.Relu,
+                        bias=b1_f[:, 4 * g + 2 * pair + s : 4 * g + 2 * pair + s + 1],
+                    )
+                if pair == 0:
+                    between()
+
+        def inter_h(g, width):
+            h_inter[g] = work("inter", [P, 512, 4], BF16, 3)
+            nc.vector.tensor_copy(
+                out=h_inter[g][:, 0:width, :].rearrange("p (c i) t -> p c t i", i=4),
+                in_=h_planes[g][:, :, 0:width].rearrange("p t (c i) -> p c t i", i=4),
+            )
+
+        def quant_h(g, n0, width):
+            nc.vector.quantize_mx(
+                out=hc[g][0][:, n0 : n0 + width].bitcast(FP8X4),
+                scales=hc[g][1][:, n0 : n0 + width],
+                in_=h_inter[g][:, 0:width, :].rearrange("p n t -> p (n t)"),
+            )
+
+        acc = {}
+
+        def stage2(g, tiles):
+            for i in tiles:
+                if g == 0:
+                    acc[i] = psum.tile([P, 512], F32, name="acc%d" % i, tag="acc%d" % i)
+                toks = slice(128 * i, 128 * i + 128)
+                nc.tensor.matmul_mx(
+                    out=acc[i][:],
+                    lhsT=hc[g][0][:, toks].bitcast(FP8X4), lhsT_scale=hc[g][1][:, toks],
+                    rhs=w2c[g][0][:].bitcast(FP8X4), rhs_scale=w2c[g][1][:],
+                    start=(g == 0), stop=(g == GROUPS - 1),
+                )
+
+        pick = kept("pick", [P, 1], BF16)
+        nc.vector.tensor_sub(out=pick[:], in0=ident_b[:, 8:9], in1=ident_b[:, 9:10])
+        res, scaled, mapped, ss, f_row, ss2, r_row = {}, {}, {}, {}, {}, {}, {}
+
+        def ep_res(half, i):
+            res[i] = work("res", [P, 512], F32, 4)
+            nc.vector.tensor_add(out=res[i][:], in0=acc[i][:], in1=b2_bc[:])
+            junk = work("junk", [P, 512], BF16, 2)
+            ss[i] = work("ss", [P, 1], F32, 4)
+            nc.scalar.activation(out=junk[:], in_=res[i][:], func=ACT.Square, accum_out=ss[i][:])
+
+        def ep_f(i):
+            clamped = work("clamped", [P, 1], F32, 4)
+            f_row[i] = work("f_row", [P, 1], F32, 4)
+            nc.gpsimd.tensor_scalar(
+                out=clamped[:], in0=ss[i][:], scalar1=inv_nm2, scalar2=1.0, op0=OP.mult, op1=OP.max
+            )
+            nc.gpsimd.tensor_tensor(out=f_row[i][:], in0=clamped[:], in1=neg_half[:], op=OP.pow)
+
+        def ep_scaled(i):
+            scaled[i] = work("scaled", [P, 512], F32, 4)
+            nc.vector.tensor_mul(out=scaled[i][:], in0=res[i][:], in1=ostd_bc[:])
+
+        def ep_mapped(half, i):
+            bank = ring()
+            nc.tensor.matmul(out=bank[:], lhsT=ident_b[:], rhs=x_sb[half, i // 2][:, i % 2, :], start=True, stop=False)
+            nc.tensor.matmul(
+                out=bank[:], lhsT=pick[:, 0:1].to_broadcast([P, P]), rhs=vecs[:], start=False, stop=True
+            )
+            mapped[i] = work("mapped", [P, 512], F32, 4)
+            nc.vector.scalar_tensor_tensor(
+                out=mapped[i][:], in0=scaled[i][:], scalar=f_row[i][:, 0:1], in1=bank[:], op0=OP.mult, op1=OP.add
+            )
+            junk = work("junk", [P, 512], BF16, 2)
+            ss2[i] = work("ss2", [P, 1], F32, 4)
+            nc.scalar.activation(out=junk[:], in_=mapped[i][:], func=ACT.Square, accum_out=ss2[i][:])
+
+        def ep_r(i):
+            clamped = work("clamped2", [P, 1], F32, 4)
+            r_row[i] = work("r_row", [P, 1], F32, 4)
+            nc.gpsimd.tensor_scalar(
+                out=clamped[:], in0=ss2[i][:], scalar1=1e-24, scalar2=0.0, op0=OP.max, op1=OP.add
+            )
+            nc.gpsimd.tensor_tensor(out=r_row[i][:], in0=clamped[:], in1=neg_half[:], op=OP.pow)
+
+        def ep_out(half, i, vector):
+            final = work("final", [P, 512], F32, 3)
+            if vector:
+                nc.vector.tensor_scalar_mul(out=final[:], in0=mapped[i][:], scalar1=r_row[i][:, 0:1])
+            else:
+                nc.scalar.activation(out=final[:], in_=mapped[i][:], func=ACT.Copy, scale=r_row[i][:, 0:1])
+            rows = out[half * HALF : (half + 1) * HALF, :].rearrange("(p i) n -> p i n", i=4)
+            nc.sync.dma_start(out=rows[:, i, :], in_=final[:])
+
+        def epilogue(unit):
+            for name in EP.get(unit, "").split():
+                half = 0 if name[0] == "a" else 1
+                i = int(name[2])
+                k = name[1]
+                if k == "R":
+                    ep_res(half, i)
+                elif k == "F":
+                    ep_f(i)
+                elif k == "Q":
+                    ep_scaled(i)
+                elif k == "M":
+                    ep_mapped(half, i)
+                elif k == "N":
+                    ep_r(i)
+                elif k == "O":
+                    ep_out(half, i, name in VOUT)
+
+        def nothing():
+            return None
+
+        xi = x_path(0, 1)
+        prep_w1(0)
+        quantize(xc[0], xi)
+        quantize(w1c[0], w1g[0])
+        bias_columns()
+        prep_w1(1)
+        quantize(w1c[1], w1g[1])
+
+        w2_step = {s: g for g, s in enumerate(W2STEPS)}
+        pass_step = {}
+        for step, g in w2_step.items():
+            pass_step[max(step, g) + 2] = g
+
+        def weights(step):
+            if step in PSTEPS:
+                scale_w2(PSTEPS.index(step))
+            if step + 2 < GROUPS:
+                prep_w1(step + 2)
+            if step in w2_step:
+                prep_w2(w2_step[step])
+
+        if -1 in PSTEPS:
+            scale_w2(0)
+        for step in range(12):
+            half, g = step // 8, step % 8
+
+            def passes():
+                if step in pass_step:
+                    stage2(pass_step[step], range(4))
+                for name in BP.get(step, "").split():
+                    stage2(int(name[0]), (int(name[1]),))
+
+            stage1(half, g, passes)
+            weights(step)
+            epilogue(step)
+            if step == XB:
+                xi = x_path(1, XBV)
+            inter_h(g, 512)
+            if step + 2 < GROUPS:
+                quantize(w1c[step + 2], w1g[step + 2])
+            quant_h(g, 0, 512)
+            if step == XB:
+                quantize(xc[1], xi)
+            if step in w2_step:
+                quantize(w2c[w2_step[step]], w2g[w2_step[step]])
+
+        for slot in range(8):
+            part, g = slot // 4, 4 + slot % 4
+
+            def passes():
+                for name in BP.get(slot + 12, "").split():
+                    stage2(int(name[0]), (int(name[1]),))
+
+            stage1_quarter(1, g, part, passes)
+            epilogue(slot + 12)
+            inter_h(g, 256)
+            quant_h(g, 256 * part, 256)
+
+        stage2(6, (2, 3))
+        stage2(7, (2, 3))
+        epilogue(20)

@@ -16,14 +16,18 @@ OP = mybir.AluOpType
 ACT = mybir.ActivationFunctionType
 
 P = 128
-W2STEPS = [0, 1, 2, 3, 5, 6, 8, 9]
-XB = 2
+W2STEPS = [0, 1, 2, 3, 4, 5, 8, 9]
+XB = 1
 XBV = 0
-PSTEPS = [0, 2, 4, 7]
-EP = {12: 'aR2 aR1 aR3 aQ1 aF2 aR0', 14: 'aF1 aQ0 aF3 aF0 aM0 aM1 aN0 aQ2', 15: 'aQ3 aM2', 16: 'aO0 aM3 aN1 aN3', 17: 'bR0 bR1 bF1 aO3 bF0 aN2', 18: 'aO1 bQ1 aO2 bQ0', 19: 'bM0 bM1', 20: 'bN0 bR2 bN1 bR3 bO0 bO1 bQ2 bF2 bM2 bQ3 bF3 bN2 bM3 bN3 bO2 bO3'}
-VOUT = ['bO2', 'bO3', 'aO3', 'bO1', 'aO0', 'bO0']
-BP = {14: '00 10 02 20 01 30 11 21', 15: '12 22 03 13 23 31 33 41', 16: '32 51 40 61', 17: '50 60 70 71', 19: '43 52 53', 18: '42'}
-LOADS = 'x0 w0 c0 w2 w1 c1 w5 c3 w7 w3 x1 w4 c2 w6'
+PCNT = {-1: 4, 0: 2, 1: 3, 2: 1, 3: 3, 6: 1, 7: 2}
+VORD = 'xi2p1qhe'
+ASTART = [12, 14, 15, 11]
+BSTART = [16, 20]
+SG = 4
+CAP = 10
+LAG = 1
+VOUTA = [0, 1, 2, 3]
+LOADS = 'x0 w0 s0 b0 w1 w2 s1 b1 x1 w3 s2 w4 w5 w6 b3 b2 w7 s3'
 GROUPS = 8
 HALF = 512
 TILES = 4
@@ -39,7 +43,7 @@ def tile_mlp_kernel(
         keep = ctx.enter_context(tc.tile_pool(name="keep", bufs=1))
         pool = ctx.enter_context(tc.tile_pool(name="work", bufs=2))
         psum = ctx.enter_context(tc.psum_pool(name="psum", bufs=1))
-        ctx.enter_context(tc.manual_schedule(engines={mybir.EngineType.PE, mybir.EngineType.SP}))
+        ctx.enter_context(tc.manual_schedule(engines={mybir.EngineType.SP}))
 
         def kept(name, shape, dtype):
             return keep.tile(shape, dtype, name=name, align_bytes=64)
@@ -76,11 +80,14 @@ def tile_mlp_kernel(
             rows = W1[512 * g : 512 * (g + 1), :].rearrange("(m t) k -> m t k", t=4)
             nc.sync.dma_start(out=w1_sb[g][:], in_=rows)
 
-        def load_w2(c):
+        def load_scale(c):
             cols = slice(1024 * c, 1024 * (c + 1))
             nc.sync.dma_start(
                 out=sc_sb[c][:], in_=W2_scale[:, cols].rearrange("o k -> (o k)").partition_broadcast(P)
             )
+
+        def load_w2(c):
+            cols = slice(1024 * c, 1024 * (c + 1))
             nc.sync.dma_start(
                 out=w2_bytes_sb[c][:], in_=W2_bytes[:, cols].rearrange("(j p) k -> p j k", p=P)
             )
@@ -94,7 +101,7 @@ def tile_mlp_kernel(
         nc.scalar.dma_start(out=vecs[8:9, :], in_=out_mean.rearrange("(o k) -> o k", o=1))
         nc.scalar.dma_start(out=vecs[9:10, :], in_=in_mean.rearrange("(o k) -> o k", o=1))
         for item in LOADS.split():
-            {"x": load_x, "w": load_w1, "c": load_w2}[item[0]](int(item[1]))
+            {"x": load_x, "w": load_w1, "b": load_w2, "s": load_scale}[item[0]](int(item[1]))
         nc.sync.dma_start(out=b2_bc[:], in_=b2.partition_broadcast(P))
         nc.sync.dma_start(out=ostd_bc[:], in_=out_std.partition_broadcast(P))
 
@@ -190,12 +197,20 @@ def tile_mlp_kernel(
                 bank = transposes(w1_sb[g][:].bitcast(F32), first)
                 copy_out(w1g[g], bank, first)
 
-        def scale_w2(c):
-            w2s[c] = work("w2s", [P, 4, 1024], BF16, 2)
-            for j in range(4):
-                nc.vector.tensor_tensor(
-                    out=w2s[c][:, j, :], in0=w2_bytes_sb[c][:, j, :].bitcast(FP8), in1=sc_sb[c][:], op=OP.mult
-                )
+        def scale_w2(piece):
+            c, j = piece // 4, piece % 4
+            if j == 0:
+                w2s[c] = work("w2s", [P, 4, 1024], BF16, 2)
+            nc.vector.tensor_tensor(
+                out=w2s[c][:, j, :], in0=w2_bytes_sb[c][:, j, :].bitcast(FP8), in1=sc_sb[c][:], op=OP.mult
+            )
+
+        pieces = [0]
+
+        def scale_next(count):
+            for n in range(count):
+                scale_w2(pieces[0])
+                pieces[0] += 1
 
         def prep_w2(g):
             w2g[g] = work("w2g", [P, 512, 4], BF16, 2)
@@ -340,23 +355,25 @@ def tile_mlp_kernel(
             rows = out[half * HALF : (half + 1) * HALF, :].rearrange("(p i) n -> p i n", i=4)
             nc.sync.dma_start(out=rows[:, i, :], in_=final[:])
 
+        def epilogue_stage(half, i, stage):
+            if stage == 0:
+                ep_res(half, i)
+            elif stage == 1:
+                ep_f(i)
+                ep_scaled(i)
+            elif stage == 2:
+                ep_mapped(half, i)
+            elif stage == 3:
+                ep_r(i)
+                ep_out(half, i, half == 1 or i in VOUTA)
+
         def epilogue(unit):
-            for name in EP.get(unit, "").split():
-                half = 0 if name[0] == "a" else 1
-                i = int(name[2])
-                k = name[1]
-                if k == "R":
-                    ep_res(half, i)
-                elif k == "F":
-                    ep_f(i)
-                elif k == "Q":
-                    ep_scaled(i)
-                elif k == "M":
-                    ep_mapped(half, i)
-                elif k == "N":
-                    ep_r(i)
-                elif k == "O":
-                    ep_out(half, i, name in VOUT)
+            for i in range(TILES):
+                assert unit != ASTART[i] or unit >= max(pass_step)
+                epilogue_stage(0, i, unit - ASTART[i])
+            for i in range(2):
+                assert unit != BSTART[i] or (7, i) not in open_passes
+                epilogue_stage(1, i, unit - BSTART[i])
 
         def nothing():
             return None
@@ -370,55 +387,70 @@ def tile_mlp_kernel(
         quantize(w1c[1], w1g[1])
 
         w2_step = {s: g for g, s in enumerate(W2STEPS)}
-        pass_step = {}
-        for step, g in w2_step.items():
-            pass_step[max(step, g) + 2] = g
+        pass_step = {max(step, g) + 2: g for step, g in w2_step.items()}
 
-        def weights(step):
-            if step in PSTEPS:
-                scale_w2(PSTEPS.index(step))
-            if step + 2 < GROUPS:
-                prep_w1(step + 2)
-            if step in w2_step:
-                prep_w2(w2_step[step])
+        scale_next(PCNT.get(-1, 0))
+        x_inter = [None]
+        units = [(0, g, 0, 512) for g in range(GROUPS)] + [(1, g, 0, 512) for g in range(SG)]
+        units += [(1, g, n0, 256) for n0 in (0, 256) for g in range(SG, GROUPS)]
+        done = {}
+        open_passes = [(g, i) for g in range(GROUPS) for i in range(TILES)]
 
-        if -1 in PSTEPS:
-            scale_w2(0)
-        for step in range(12):
-            half, g = step // 8, step % 8
+        def passes_b(unit):
+            count = 0
+            for g, i in list(open_passes):
+                ready = max(done.get((g, 128 * i), 99), ASTART[i])
+                if count < CAP and ready + LAG <= unit and all((q, i) not in open_passes for q in range(g)):
+                    stage2(g, (i,))
+                    open_passes.remove((g, i))
+                    count += 1
 
-            def passes():
-                if step in pass_step:
-                    stage2(pass_step[step], range(4))
-                for name in BP.get(step, "").split():
-                    stage2(int(name[0]), (int(name[1]),))
-
-            stage1(half, g, passes)
-            weights(step)
-            epilogue(step)
-            if step == XB:
-                xi = x_path(1, XBV)
-            inter_h(g, 512)
-            if step + 2 < GROUPS:
-                quantize(w1c[step + 2], w1g[step + 2])
-            quant_h(g, 0, 512)
-            if step == XB:
-                quantize(xc[1], xi)
-            if step in w2_step:
-                quantize(w2c[w2_step[step]], w2g[w2_step[step]])
-
-        for slot in range(8):
-            part, g = slot // 4, 4 + slot % 4
+        for unit, (half, g, n0, width) in enumerate(units):
 
             def passes():
-                for name in BP.get(slot + 12, "").split():
-                    stage2(int(name[0]), (int(name[1]),))
+                if unit in pass_step:
+                    stage2(pass_step[unit], range(4))
+                if half == 1:
+                    passes_b(unit)
 
-            stage1_quarter(1, g, part, passes)
-            epilogue(slot + 12)
-            inter_h(g, 256)
-            quant_h(g, 256 * part, 256)
+            if width == 512:
+                stage1(half, g, passes)
+            else:
+                stage1_quarter(half, g, n0 // 256, passes)
+            if unit + 2 < GROUPS:
+                prep_w1(unit + 2)
+            if unit in w2_step:
+                prep_w2(w2_step[unit])
+            if unit == XB:
+                x_inter[0] = x_path(1, XBV)
+            count = PCNT.get(unit, 0)
+            for item in VORD:
+                if item == "e":
+                    epilogue(unit)
+                if item == "p":
+                    scale_next((count + 1) // 2)
+                if item == "q":
+                    scale_next(count // 2)
+                if item == "i":
+                    inter_h(g, width)
+                if item == "1" and unit + 2 < GROUPS:
+                    quantize(w1c[unit + 2], w1g[unit + 2])
+                if item == "h":
+                    quant_h(g, n0, width)
+                    if half == 1:
+                        for q in range(n0, n0 + width, 128):
+                            done[g, q] = unit
+                if item == "x" and unit == XB:
+                    quantize(xc[1], x_inter[0])
+                if item == "2" and unit in w2_step:
+                    quantize(w2c[w2_step[unit]], w2g[w2_step[unit]])
 
-        stage2(6, (2, 3))
-        stage2(7, (2, 3))
-        epilogue(20)
+        for g, i in list(open_passes):
+            stage2(g, (i,))
+        last = len(units)
+        assert max(ASTART) + 3 < last and all(BSTART[i] > ASTART[i] + 3 for i in range(2))
+        for stage in range(4):
+            for i in range(TILES):
+                start = BSTART[i] if i < 2 else last
+                if start + stage >= last:
+                    epilogue_stage(1, i, stage)

@@ -16,34 +16,30 @@ OP = mybir.AluOpType
 ACT = mybir.ActivationFunctionType
 
 P = 128
-W2STEPS = [0, 1, 2, 3, 4, 5, 8, 9]
-XB = 1
-XBV = 0
-PCNT = {-1: 4, 0: 2, 1: 3, 2: 1, 3: 3, 6: 1, 7: 2}
-VORD = 'xi2p1qhe'
-ASTART = [12, 14, 15, 11]
-BSTART = [16, 20]
-SG = 4
-CAP = 10
-LAG = 1
-VOUTA = [0, 1, 2, 3]
-LOADS = 'x0 w0 s0 b0 w1 w2 s1 b1 x1 w3 s2 w4 w5 w6 b3 b2 w7 s3'
-GROUPS = 8
-HALF = 512
-TILES = 4
+GROUP = 512
+GROUPS = D_HID // GROUP
+HALF = B // 2
+TILES = HALF // P
+CHUNK = 2 * GROUP
+EPS_SQUARED = 1e-24
+
+LAST_STRETCH = (
+    "h a r0 r1 b4 r2 i r3 s0 k s2 b5 m0 z4 s1 z5 m1 r4 m2 o1 b7 s3 r5 o0 s4 o2 m3 s5 m4 b6 z6 z7 r6 r7 m5 o4 s6 o3 "
+    "s7 m6 m7 o5 o6 o7"
+)
 
 
 def tile_mlp_kernel(
     tc, x, in_mean, in_std, out_mean, out_std, W1, b1, W2_bytes, W2_scale, b2, norm_max, out
 ):
     nc = tc.nc
-    inv_nm2 = 1.0 / (float(norm_max) * float(norm_max))
+    inverse_square_of_norm_max = 1.0 / (float(norm_max) * float(norm_max))
 
     with ExitStack() as ctx:
         keep = ctx.enter_context(tc.tile_pool(name="keep", bufs=1))
         pool = ctx.enter_context(tc.tile_pool(name="work", bufs=2))
         psum = ctx.enter_context(tc.psum_pool(name="psum", bufs=1))
-        ctx.enter_context(tc.manual_schedule(engines={mybir.EngineType.SP}))
+        ctx.enter_context(tc.manual_schedule())
 
         def kept(name, shape, dtype):
             return keep.tile(shape, dtype, name=name, align_bytes=64)
@@ -51,406 +47,389 @@ def tile_mlp_kernel(
         def work(tag, shape, dtype, bufs):
             return pool.tile(shape, dtype, name=tag, tag=tag, bufs=bufs, align_bytes=64)
 
-        ring_next = [0]
+        banks_used = [0]
 
-        def ring():
-            tag = "ring%d" % (ring_next[0] % 4)
-            ring_next[0] += 1
+        def next_bank():
+            tag = "ring%d" % (banks_used[0] % 4)
+            banks_used[0] += 1
             return psum.tile([P, 512], F32, name=tag, tag=tag)
 
-        mean_col = kept("mean_col", [P, 4], BF16)
-        std_col = kept("std_col", [P, 4], BF16)
-        vecs = kept("vecs", [P, 512], BF16)
-        x_sb = {}
+        in_mean_columns = kept("in_mean_columns", [P, 4], BF16)
+        in_std_columns = kept("in_std_columns", [P, 4], BF16)
+        b1_rows = kept("b1_rows", [P, 512], BF16)
+        mean_rows = kept("mean_rows", [P, 512], BF16)
+        b2_everywhere = kept("b2_everywhere", [P, D_OUT], BF16)
+        out_std_everywhere = kept("out_std_everywhere", [P, D_OUT], BF16)
+        x_rows = {}
         for half in range(2):
             for pair in range(2):
-                x_sb[half, pair] = kept("x_sb%d%d" % (half, pair), [P, 2, D_IN], BF16)
-        w1_sb = [kept("w1_sb%d" % g, [P, 4, D_IN], BF16) for g in range(GROUPS)]
-        sc_sb = [kept("sc_sb%d" % c, [P, 1024], F32) for c in range(4)]
-        w2_bytes_sb = [kept("w2_bytes_sb%d" % c, [P, 4, 1024], U8) for c in range(4)]
-        b2_bc = kept("b2_bc", [P, D_OUT], BF16)
-        ostd_bc = kept("ostd_bc", [P, D_OUT], BF16)
+                x_rows[half, pair] = kept("x_rows%d%d" % (half, pair), [P, 2, D_IN], BF16)
+        w1_rows, w2_bytes, w2_scales = {}, {}, {}
 
         def load_x(half):
-            rows = x[half * HALF : (half + 1) * HALF, :].rearrange("(p i) k -> p i k", i=4)
+            rows = x[half * HALF : (half + 1) * HALF, :].rearrange("(q i) k -> q i k", i=TILES)
             for pair in range(2):
-                nc.sync.dma_start(out=x_sb[half, pair][:], in_=rows[:, 2 * pair : 2 * pair + 2, :])
+                nc.sync.dma_start(out=x_rows[half, pair][:], in_=rows[:, 2 * pair : 2 * pair + 2, :])
 
         def load_w1(g):
-            rows = W1[512 * g : 512 * (g + 1), :].rearrange("(m t) k -> m t k", t=4)
-            nc.sync.dma_start(out=w1_sb[g][:], in_=rows)
-
-        def load_scale(c):
-            cols = slice(1024 * c, 1024 * (c + 1))
+            w1_rows[g] = work("w1_rows", [P, 4, D_IN], BF16, 4)
             nc.sync.dma_start(
-                out=sc_sb[c][:], in_=W2_scale[:, cols].rearrange("o k -> (o k)").partition_broadcast(P)
+                out=w1_rows[g][:], in_=W1[GROUP * g : GROUP * (g + 1), :].rearrange("(m t) k -> m t k", t=4)
             )
 
-        def load_w2(c):
-            cols = slice(1024 * c, 1024 * (c + 1))
-            nc.sync.dma_start(
-                out=w2_bytes_sb[c][:], in_=W2_bytes[:, cols].rearrange("(j p) k -> p j k", p=P)
-            )
+        def load_w2_scales(c):
+            w2_scales[c] = work("w2_scales", [P, CHUNK], F32, 2)
+            row = W2_scale[:, CHUNK * c : CHUNK * (c + 1)].rearrange("o k -> (o k)")
+            nc.sync.dma_start(out=w2_scales[c][:], in_=row.partition_broadcast(P))
 
-        nc.vector.memset(vecs[:], 0.0)
-        warm = kept("warm", [P, 1], F32)
-        nc.vector.memset(warm[:], 0.0)
-        nc.scalar.dma_start(out=mean_col[:], in_=in_mean.rearrange("(p t) -> p t", t=4))
-        nc.scalar.dma_start(out=std_col[:], in_=in_std.rearrange("(p t) -> p t", t=4))
-        nc.scalar.dma_start(out=vecs[0:8, :], in_=b1.rearrange("(g k) -> g k", g=GROUPS))
-        nc.scalar.dma_start(out=vecs[8:9, :], in_=out_mean.rearrange("(o k) -> o k", o=1))
-        nc.scalar.dma_start(out=vecs[9:10, :], in_=in_mean.rearrange("(o k) -> o k", o=1))
-        for item in LOADS.split():
-            {"x": load_x, "w": load_w1, "b": load_w2, "s": load_scale}[item[0]](int(item[1]))
-        nc.sync.dma_start(out=b2_bc[:], in_=b2.partition_broadcast(P))
-        nc.sync.dma_start(out=ostd_bc[:], in_=out_std.partition_broadcast(P))
+        def load_w2_bytes(c):
+            w2_bytes[c] = work("w2_bytes", [P, 4, CHUNK], U8, 2)
+            columns = W2_bytes[:, CHUNK * c : CHUNK * (c + 1)]
+            nc.sync.dma_start(out=w2_bytes[c][:], in_=columns.rearrange("(j q) k -> q j k", q=P))
 
-        ident_f = kept("ident_f", [P, P], F32)
-        make_identity(nc, ident_f[:])
-        ident_b = kept("ident_b", [P, P], BF16)
-        make_identity(nc, ident_b[:])
-        neg_half = kept("neg_half", [P, 1], F32)
-        nc.gpsimd.memset(neg_half[:], -0.5)
+        nc.vector.memset(b1_rows[:], 0.0)
+        nc.gpsimd.memset(mean_rows[:], 0.0)
+        scratch = kept("scratch", [P, 1], F32)
+        nc.vector.memset(scratch[:], 0.0)
 
-        nc.scalar.activation(out=warm[:], in_=warm[:], func=ACT.Relu)
+        load_x(0)
+        nc.sync.dma_start(out=in_mean_columns[:], in_=in_mean.rearrange("(p t) -> p t", t=4))
+        nc.sync.dma_start(out=in_std_columns[:], in_=in_std.rearrange("(p t) -> p t", t=4))
+        load_w1(0)
+        nc.sync.dma_start(out=b1_rows[0:GROUPS, :], in_=b1.rearrange("(g k) -> g k", g=GROUPS))
+        load_w2_bytes(0)
+        load_w2_scales(0)
+        load_w1(1)
+        load_x(1)
+        load_w1(2)
+        load_w2_bytes(1)
+        load_w2_scales(1)
+        load_w1(3)
+
+        def load_epilogue_rows():
+            nc.sync.dma_start(out=mean_rows[0:1, :], in_=out_mean.rearrange("(o k) -> o k", o=1))
+            nc.sync.dma_start(out=mean_rows[1:2, :], in_=in_mean.rearrange("(o k) -> o k", o=1))
+            nc.sync.dma_start(out=b2_everywhere[:], in_=b2.partition_broadcast(P))
+            nc.sync.dma_start(out=out_std_everywhere[:], in_=out_std.partition_broadcast(P))
+
+        identity = kept("identity", [P, P], F32)
+        make_identity(nc, identity[:])
+        identity_bf16 = kept("identity_bf16", [P, P], BF16)
+        make_identity(nc, identity_bf16[:])
+        minus_half = kept("minus_half", [P, 1], F32)
+        nc.gpsimd.memset(minus_half[:], -0.5)
+        nc.scalar.activation(out=scratch[:], in_=scratch[:], func=ACT.Relu)
 
         def codes(name):
             return kept(name + "_codes", [P, 512], U32), kept(name + "_scales", [P, 512], U8)
 
-        xc = [codes("xc%d" % h) for h in range(2)]
-        w1c = [codes("w1c%d" % g) for g in range(GROUPS)]
-        w2c = [codes("w2c%d" % g) for g in range(GROUPS)]
-        hc = [codes("hc%d" % g) for g in range(GROUPS)]
+        x_codes = [codes("x%d" % half) for half in range(2)]
+        w1_codes = [codes("w1_%d" % g) for g in range(GROUPS)]
+        w2_codes = [codes("w2_%d" % g) for g in range(GROUPS)]
+        h_codes = [[codes("h%d_%d" % (half, g)) for g in range(GROUPS)] for half in range(2)]
 
-        def quantize(dst, src, cols=slice(0, 512)):
+        def quantize(operand, slots):
             nc.vector.quantize_mx(
-                out=dst[0][:, cols].bitcast(FP8X4),
-                scales=dst[1][:, cols],
-                in_=src[:].rearrange("p n t -> p (n t)"),
+                out=operand[0][:].bitcast(FP8X4), scales=operand[1][:], in_=slots[:].rearrange("p n t -> p (n t)")
             )
 
+        def interleave(slots, planes):
+            nc.vector.tensor_copy(
+                out=slots.rearrange("p (c i) t -> p c t i", i=4), in_=planes.rearrange("p t (c i) -> p c t i", i=4)
+            )
 
-        rstd = kept("rstd", [P, 4], F32)
-        mean_f = kept("mean_f", [P, 4], F32)
-        nmr = kept("nmr", [P, 4], F32)
-        nc.vector.reciprocal(out=rstd[:], in_=std_col[:])
-        nc.vector.tensor_copy(out=mean_f[:], in_=mean_col[:])
+        in_rstd = kept("in_rstd", [P, 4], F32)
+        in_mean_f32 = kept("in_mean_f32", [P, 4], F32)
+        in_shift = kept("in_shift", [P, 4], F32)
+        nc.vector.reciprocal(out=in_rstd[:], in_=in_std_columns[:])
+        nc.vector.tensor_copy(out=in_mean_f32[:], in_=in_mean_columns[:])
         nc.vector.scalar_tensor_tensor(
-            out=nmr[:], in0=mean_col[:], scalar=-1.0, in1=rstd[:], op0=OP.mult, op1=OP.mult
+            out=in_shift[:], in0=in_mean_columns[:], scalar=-1.0, in1=in_rstd[:], op0=OP.mult, op1=OP.mult
         )
+        mean_picker = kept("mean_picker", [P, 1], BF16)
+        nc.vector.tensor_sub(out=mean_picker[:], in0=identity_bf16[:, 0:1], in1=identity_bf16[:, 1:2])
 
-        def x_path(half, vector_u):
-            planes = work("planes", [P, 4, 512], BF16, 3)
-            inter = work("inter", [P, 512, 4], BF16, 3)
-            for pair in range(2):
-                bank = ring()
-                words = x_sb[half, pair][:].bitcast(F32)
-                for u in range(2):
-                    for i in range(2):
-                        col = 256 * u + 128 * i
-                        nc.tensor.transpose(bank[:, col : col + 128], words[:, i, u:256:2], ident_f[:])
-                toks = slice(256 * pair, 256 * pair + 256)
-                for t in range(4):
-                    u, e = t // 2, t % 2
-                    src = bank[:, 256 * u : 256 * u + 256].bitcast(BF16).rearrange("p (n e) -> p e n", e=2)[:, e, :]
-                    if pair < vector_u:
-                        nc.vector.tensor_scalar(
-                            out=planes[:, t, toks], in0=src, scalar1=mean_f[:, t : t + 1],
-                            scalar2=rstd[:, t : t + 1], op0=OP.subtract, op1=OP.mult,
-                        )
-                    else:
-                        nc.scalar.activation(
-                            out=planes[:, t, toks], in_=src, func=ACT.Identity,
-                            scale=rstd[:, t : t + 1], bias=nmr[:, t : t + 1],
-                        )
-            for pair in range(2):
-                toks = slice(256 * pair, 256 * pair + 256)
-                nc.vector.tensor_copy(
-                    out=inter[:, toks, :].rearrange("p (c i) t -> p c t i", i=4),
-                    in_=planes[:, :, toks].rearrange("p t (c i) -> p c t i", i=4),
-                )
-            return inter
+        x_planes, x_slots = {}, {}
 
-        w1g = {}
-        w2s = {}
-        w2g = {}
+        def normalise_x(half, pair):
+            if pair == 0:
+                x_planes[half] = work("planes", [P, 4, 512], BF16, 3)
+                x_slots[half] = work("slots", [P, 512, 4], BF16, 3)
+            bank = next_bank()
+            words = x_rows[half, pair][:].bitcast(F32)
+            for u in range(2):
+                for i in range(2):
+                    first = 256 * u + 128 * i
+                    nc.tensor.transpose(bank[:, first : first + 128], words[:, i, u:256:2], identity[:])
+            tokens = slice(256 * pair, 256 * pair + 256)
+            for t in range(4):
+                u, e = t // 2, t % 2
+                both = bank[:, 256 * u : 256 * u + 256].bitcast(BF16).rearrange("p (n e) -> p e n", e=2)
+                if pair == 1:
+                    nc.vector.tensor_scalar(
+                        out=x_planes[half][:, t, tokens],
+                        in0=both[:, e, :],
+                        scalar1=in_mean_f32[:, t : t + 1],
+                        scalar2=in_rstd[:, t : t + 1],
+                        op0=OP.subtract,
+                        op1=OP.mult,
+                    )
+                else:
+                    nc.scalar.activation(
+                        out=x_planes[half][:, t, tokens],
+                        in_=both[:, e, :],
+                        func=ACT.Identity,
+                        scale=in_rstd[:, t : t + 1],
+                        bias=in_shift[:, t : t + 1],
+                    )
 
-        def transposes(words4, first):
-            bank = ring()
+        def interleave_x(half, pair):
+            tokens = slice(256 * pair, 256 * pair + 256)
+            interleave(x_slots[half][:, tokens, :], x_planes[half][:, :, tokens])
+
+        w1_slots, w2_scaled, w2_slots = {}, {}, {}
+
+        def turn(slots, words, first):
+            bank = next_bank()
             for s in range(2):
                 for u in range(2):
-                    col = 256 * s + 128 * u
-                    nc.tensor.transpose(bank[:, col : col + 128], words4[:, first + s, u:256:2], ident_f[:])
-            return bank
-
-        def copy_out(dst, bank, first):
+                    column = 256 * s + 128 * u
+                    nc.tensor.transpose(bank[:, column : column + 128], words[:, first + s, u:256:2], identity[:])
             nc.scalar.copy(
-                out=dst[:].bitcast(F32)[:, 128 * first : 128 * first + 256, :].rearrange(
-                    "p (s m) u -> p s m u", s=2
-                ),
+                out=slots[:].bitcast(F32)[:, 128 * first : 128 * first + 256, :].rearrange("p (s m) u -> p s m u", s=2),
                 in_=bank[:].rearrange("p (s u m) -> p s m u", s=2, u=2),
             )
 
-        def prep_w1(g):
-            w1g[g] = work("w1g", [P, 512, 4], BF16, 2)
+        def turn_w1(g):
+            w1_slots[g] = work("w1_slots", [P, 512, 4], BF16, 2)
             for first in (0, 2):
-                bank = transposes(w1_sb[g][:].bitcast(F32), first)
-                copy_out(w1g[g], bank, first)
+                turn(w1_slots[g], w1_rows[g][:].bitcast(F32), first)
+            if g + 4 < GROUPS:
+                load_w1(g + 4)
 
-        def scale_w2(piece):
-            c, j = piece // 4, piece % 4
+        scaled_rows = [0]
+
+        def scale_w2_row():
+            c, j = scaled_rows[0] // 4, scaled_rows[0] % 4
             if j == 0:
-                w2s[c] = work("w2s", [P, 4, 1024], BF16, 2)
+                w2_scaled[c] = work("w2_scaled", [P, 4, CHUNK], BF16, 2)
             nc.vector.tensor_tensor(
-                out=w2s[c][:, j, :], in0=w2_bytes_sb[c][:, j, :].bitcast(FP8), in1=sc_sb[c][:], op=OP.mult
+                out=w2_scaled[c][:, j, :], in0=w2_bytes[c][:, j, :].bitcast(FP8), in1=w2_scales[c][:], op=OP.mult
             )
+            scaled_rows[0] += 1
+            if j == 3 and c + 2 < D_HID // CHUNK:
+                load_w2_scales(c + 2)
+                load_w2_bytes(c + 2)
 
-        pieces = [0]
-
-        def scale_next(count):
-            for n in range(count):
-                scale_w2(pieces[0])
-                pieces[0] += 1
-
-        def prep_w2(g):
-            w2g[g] = work("w2g", [P, 512, 4], BF16, 2)
+        def turn_w2(g):
+            w2_slots[g] = work("w2_slots", [P, 512, 4], BF16, 2)
+            words = w2_scaled[g // 2][:].bitcast(F32)[:, :, 256 * (g % 2) : 256 * (g % 2) + 256]
             for first in (0, 2):
-                bank = transposes(w2s[g // 2][:].bitcast(F32)[:, :, 256 * (g % 2) : 256 * (g % 2) + 256], first)
-                copy_out(w2g[g], bank, first)
+                turn(w2_slots[g], words, first)
 
-        b1_f = kept("b1_f", [P, 32], F32)
+        b1_words = kept("b1_words", [P, GROUPS, 2], F32)
+        b1_columns = kept("b1_columns", [P, 4 * GROUPS], F32)
 
-        def bias_columns():
-            bank = ring()
-            words = vecs[:].bitcast(F32)
+        def turn_b1():
+            bank = next_bank()
+            words = b1_rows[:].bitcast(F32)
             for u in range(2):
-                nc.tensor.transpose(bank[:, 128 * u : 128 * u + 128], words[:, u:256:2], ident_f[:])
-            b1_w = kept("b1_w", [P, 8, 2], F32)
+                nc.tensor.transpose(bank[:, 128 * u : 128 * u + 128], words[:, u:256:2], identity[:])
             nc.vector.tensor_copy(
-                out=b1_w[:], in_=bank[:, 0:256].rearrange("p (u g) -> p g u", u=2)[:, 0:8, :]
+                out=b1_words[:], in_=bank[:, 0:256].rearrange("p (u g) -> p g u", u=2)[:, 0:GROUPS, :]
             )
-            nc.vector.tensor_copy(out=b1_f[:], in_=b1_w[:].rearrange("p g u -> p (g u)").bitcast(BF16))
+            nc.vector.tensor_copy(out=b1_columns[:], in_=b1_words[:].rearrange("p g u -> p (g u)").bitcast(BF16))
 
-        h_planes = {}
-        h_inter = {}
+        h_planes, h_slots = {}, {}
 
-        def matmul1(half, g, t, bank, cols, n0, n):
-            lanes = slice(128 * t, 128 * t + 128)
-            nc.tensor.matmul_mx(
-                out=bank[:, cols],
-                lhsT=w1c[g][0][:, lanes].bitcast(FP8X4), lhsT_scale=w1c[g][1][:, lanes],
-                rhs=xc[half][0][:, n0 : n0 + n].bitcast(FP8X4), rhs_scale=xc[half][1][:, n0 : n0 + n],
-                start=True, stop=True,
-            )
-
-        def relu(planes, t, g, bank, cols):
-            nc.scalar.activation(
-                out=planes[:, t, :], in_=bank[:, cols], func=ACT.Relu, bias=b1_f[:, 4 * g + t : 4 * g + t + 1]
-            )
-
-        def stage1(half, g, between):
-            planes = work("planes", [P, 4, 512], BF16, 3)
-            h_planes[g] = planes
+        def first_layer(half, g):
+            h_planes[half, g] = work("planes", [P, 4, 512], BF16, 3)
             for t in range(4):
-                bank = ring()
-                matmul1(half, g, t, bank, slice(0, 512), 0, 512)
-                relu(planes, t, g, bank, slice(0, 512))
-                if t == 1:
-                    between()
-
-        def stage1_quarter(half, g, part, between):
-            planes = work("planes", [P, 4, 512], BF16, 3)
-            h_planes[g] = planes
-            for pair in range(2):
-                bank = ring()
-                for s in range(2):
-                    matmul1(half, g, 2 * pair + s, bank, slice(256 * s, 256 * s + 256), 256 * part, 256)
-                for s in range(2):
-                    nc.scalar.activation(
-                        out=planes[:, 2 * pair + s, 0:256], in_=bank[:, 256 * s : 256 * s + 256], func=ACT.Relu,
-                        bias=b1_f[:, 4 * g + 2 * pair + s : 4 * g + 2 * pair + s + 1],
-                    )
-                if pair == 0:
-                    between()
-
-        def inter_h(g, width):
-            h_inter[g] = work("inter", [P, 512, 4], BF16, 3)
-            nc.vector.tensor_copy(
-                out=h_inter[g][:, 0:width, :].rearrange("p (c i) t -> p c t i", i=4),
-                in_=h_planes[g][:, :, 0:width].rearrange("p t (c i) -> p c t i", i=4),
-            )
-
-        def quant_h(g, n0, width):
-            nc.vector.quantize_mx(
-                out=hc[g][0][:, n0 : n0 + width].bitcast(FP8X4),
-                scales=hc[g][1][:, n0 : n0 + width],
-                in_=h_inter[g][:, 0:width, :].rearrange("p n t -> p (n t)"),
-            )
-
-        acc = {}
-
-        def stage2(g, tiles):
-            for i in tiles:
-                if g == 0:
-                    acc[i] = psum.tile([P, 512], F32, name="acc%d" % i, tag="acc%d" % i)
-                toks = slice(128 * i, 128 * i + 128)
+                bank = next_bank()
+                channels = slice(128 * t, 128 * t + 128)
                 nc.tensor.matmul_mx(
-                    out=acc[i][:],
-                    lhsT=hc[g][0][:, toks].bitcast(FP8X4), lhsT_scale=hc[g][1][:, toks],
-                    rhs=w2c[g][0][:].bitcast(FP8X4), rhs_scale=w2c[g][1][:],
-                    start=(g == 0), stop=(g == GROUPS - 1),
+                    out=bank[:],
+                    lhsT=w1_codes[g][0][:, channels].bitcast(FP8X4),
+                    lhsT_scale=w1_codes[g][1][:, channels],
+                    rhs=x_codes[half][0][:].bitcast(FP8X4),
+                    rhs_scale=x_codes[half][1][:],
+                    start=True,
+                    stop=True,
+                )
+                nc.scalar.activation(
+                    out=h_planes[half, g][:, t, :],
+                    in_=bank[:],
+                    func=ACT.Relu,
+                    bias=b1_columns[:, 4 * g + t : 4 * g + t + 1],
                 )
 
-        pick = kept("pick", [P, 1], BF16)
-        nc.vector.tensor_sub(out=pick[:], in0=ident_b[:, 8:9], in1=ident_b[:, 9:10])
-        res, scaled, mapped, ss, f_row, ss2, r_row = {}, {}, {}, {}, {}, {}, {}
+        def interleave_h(half, g):
+            h_slots[half, g] = work("slots", [P, 512, 4], BF16, 3)
+            interleave(h_slots[half, g][:], h_planes[half, g][:])
 
-        def ep_res(half, i):
-            res[i] = work("res", [P, 512], F32, 4)
-            nc.vector.tensor_add(out=res[i][:], in0=acc[i][:], in1=b2_bc[:])
-            junk = work("junk", [P, 512], BF16, 2)
-            ss[i] = work("ss", [P, 1], F32, 4)
-            nc.scalar.activation(out=junk[:], in_=res[i][:], func=ACT.Square, accum_out=ss[i][:])
+        sums = {}
 
-        def ep_f(i):
-            clamped = work("clamped", [P, 1], F32, 4)
-            f_row[i] = work("f_row", [P, 1], F32, 4)
-            nc.gpsimd.tensor_scalar(
-                out=clamped[:], in0=ss[i][:], scalar1=inv_nm2, scalar2=1.0, op0=OP.mult, op1=OP.max
+        def second_layer(half, g, i):
+            if g == 0:
+                sums[i] = psum.tile([P, 512], F32, name="sums%d" % i, tag="sums%d" % i)
+            tokens = slice(128 * i, 128 * i + 128)
+            nc.tensor.matmul_mx(
+                out=sums[i][:],
+                lhsT=h_codes[half][g][0][:, tokens].bitcast(FP8X4),
+                lhsT_scale=h_codes[half][g][1][:, tokens],
+                rhs=w2_codes[g][0][:].bitcast(FP8X4),
+                rhs_scale=w2_codes[g][1][:],
+                start=(g == 0),
+                stop=(g == GROUPS - 1),
             )
-            nc.gpsimd.tensor_tensor(out=f_row[i][:], in0=clamped[:], in1=neg_half[:], op=OP.pow)
 
-        def ep_scaled(i):
-            scaled[i] = work("scaled", [P, 512], F32, 4)
-            nc.vector.tensor_mul(out=scaled[i][:], in0=res[i][:], in1=ostd_bc[:])
+        res, scaled, mapped, res_squares, clamp, mapped_squares, reciprocal_norm = {}, {}, {}, {}, {}, {}, {}
 
-        def ep_mapped(half, i):
-            bank = ring()
-            nc.tensor.matmul(out=bank[:], lhsT=ident_b[:], rhs=x_sb[half, i // 2][:, i % 2, :], start=True, stop=False)
+        def row_squares(tile, name):
+            squares = work("squares", [P, 512], BF16, 2)
+            total = work(name, [P, 1], F32, 4)
+            nc.scalar.activation(out=squares[:], in_=tile[:], func=ACT.Square, accum_out=total[:])
+            return total
+
+        def add_bias(half, i):
+            res[half, i] = work("res", [P, 512], F32, 4)
+            nc.vector.tensor_add(out=res[half, i][:], in0=sums[i][:], in1=b2_everywhere[:])
+            res_squares[half, i] = row_squares(res[half, i], "res_squares")
+
+        def scale_out(half, i):
+            scaled[half, i] = work("scaled", [P, 512], F32, 4)
+            nc.vector.tensor_mul(out=scaled[half, i][:], in0=res[half, i][:], in1=out_std_everywhere[:])
+            ratio = work("ratio", [P, 1], F32, 4)
+            clamp[half, i] = work("clamp", [P, 1], F32, 4)
+            nc.gpsimd.tensor_scalar(
+                out=ratio[:],
+                in0=res_squares[half, i][:],
+                scalar1=inverse_square_of_norm_max,
+                scalar2=1.0,
+                op0=OP.mult,
+                op1=OP.max,
+            )
+            nc.gpsimd.tensor_tensor(out=clamp[half, i][:], in0=ratio[:], in1=minus_half[:], op=OP.pow)
+
+        def add_residual(half, i):
+            bank = next_bank()
             nc.tensor.matmul(
-                out=bank[:], lhsT=pick[:, 0:1].to_broadcast([P, P]), rhs=vecs[:], start=False, stop=True
+                out=bank[:], lhsT=identity_bf16[:], rhs=x_rows[half, i // 2][:, i % 2, :], start=True, stop=False
             )
-            mapped[i] = work("mapped", [P, 512], F32, 4)
+            nc.tensor.matmul(
+                out=bank[:], lhsT=mean_picker[:, 0:1].to_broadcast([P, P]), rhs=mean_rows[:], start=False, stop=True
+            )
+            mapped[half, i] = work("mapped", [P, 512], F32, 4)
             nc.vector.scalar_tensor_tensor(
-                out=mapped[i][:], in0=scaled[i][:], scalar=f_row[i][:, 0:1], in1=bank[:], op0=OP.mult, op1=OP.add
+                out=mapped[half, i][:],
+                in0=scaled[half, i][:],
+                scalar=clamp[half, i][:, 0:1],
+                in1=bank[:],
+                op0=OP.mult,
+                op1=OP.add,
             )
-            junk = work("junk", [P, 512], BF16, 2)
-            ss2[i] = work("ss2", [P, 1], F32, 4)
-            nc.scalar.activation(out=junk[:], in_=mapped[i][:], func=ACT.Square, accum_out=ss2[i][:])
+            mapped_squares[half, i] = row_squares(mapped[half, i], "mapped_squares")
 
-        def ep_r(i):
-            clamped = work("clamped2", [P, 1], F32, 4)
-            r_row[i] = work("r_row", [P, 1], F32, 4)
+        def divide_and_store(half, i):
+            floored = work("floored", [P, 1], F32, 4)
+            reciprocal_norm[half, i] = work("reciprocal_norm", [P, 1], F32, 4)
             nc.gpsimd.tensor_scalar(
-                out=clamped[:], in0=ss2[i][:], scalar1=1e-24, scalar2=0.0, op0=OP.max, op1=OP.add
+                out=floored[:],
+                in0=mapped_squares[half, i][:],
+                scalar1=EPS_SQUARED,
+                scalar2=0.0,
+                op0=OP.max,
+                op1=OP.add,
             )
-            nc.gpsimd.tensor_tensor(out=r_row[i][:], in0=clamped[:], in1=neg_half[:], op=OP.pow)
-
-        def ep_out(half, i, vector):
+            nc.gpsimd.tensor_tensor(out=reciprocal_norm[half, i][:], in0=floored[:], in1=minus_half[:], op=OP.pow)
             final = work("final", [P, 512], F32, 3)
-            if vector:
-                nc.vector.tensor_scalar_mul(out=final[:], in0=mapped[i][:], scalar1=r_row[i][:, 0:1])
+            if half == 1:
+                nc.vector.tensor_scalar_mul(
+                    out=final[:], in0=mapped[half, i][:], scalar1=reciprocal_norm[half, i][:, 0:1]
+                )
             else:
-                nc.scalar.activation(out=final[:], in_=mapped[i][:], func=ACT.Copy, scale=r_row[i][:, 0:1])
-            rows = out[half * HALF : (half + 1) * HALF, :].rearrange("(p i) n -> p i n", i=4)
+                nc.scalar.activation(
+                    out=final[:], in_=mapped[half, i][:], func=ACT.Copy, scale=reciprocal_norm[half, i][:, 0:1]
+                )
+            rows = out[half * HALF : (half + 1) * HALF, :].rearrange("(q i) n -> q i n", i=TILES)
             nc.sync.dma_start(out=rows[:, i, :], in_=final[:])
 
-        def epilogue_stage(half, i, stage):
-            if stage == 0:
-                ep_res(half, i)
-            elif stage == 1:
-                ep_f(i)
-                ep_scaled(i)
-            elif stage == 2:
-                ep_mapped(half, i)
-            elif stage == 3:
-                ep_r(i)
-                ep_out(half, i, half == 1 or i in VOUTA)
+        normalise_x(0, 0)
+        normalise_x(0, 1)
+        turn_w1(0)
+        interleave_x(0, 1)
+        turn_b1()
+        interleave_x(0, 0)
+        quantize(x_codes[0], x_slots[0])
+        quantize(w1_codes[0], w1_slots[0])
+        scale_w2_row()
+        scale_w2_row()
+        scale_w2_row()
+        turn_w1(1)
+        scale_w2_row()
+        quantize(w1_codes[1], w1_slots[1])
+        scale_w2_row()
+        scale_w2_row()
 
-        def epilogue(unit):
-            for i in range(TILES):
-                assert unit != ASTART[i] or unit >= max(pass_step)
-                epilogue_stage(0, i, unit - ASTART[i])
-            for i in range(2):
-                assert unit != BSTART[i] or (7, i) not in open_passes
-                epilogue_stage(1, i, unit - BSTART[i])
-
-        def nothing():
-            return None
-
-        xi = x_path(0, 1)
-        prep_w1(0)
-        quantize(xc[0], xi)
-        quantize(w1c[0], w1g[0])
-        bias_columns()
-        prep_w1(1)
-        quantize(w1c[1], w1g[1])
-
-        w2_step = {s: g for g, s in enumerate(W2STEPS)}
-        pass_step = {max(step, g) + 2: g for step, g in w2_step.items()}
-
-        scale_next(PCNT.get(-1, 0))
-        x_inter = [None]
-        units = [(0, g, 0, 512) for g in range(GROUPS)] + [(1, g, 0, 512) for g in range(SG)]
-        units += [(1, g, n0, 256) for n0 in (0, 256) for g in range(SG, GROUPS)]
-        done = {}
-        open_passes = [(g, i) for g in range(GROUPS) for i in range(TILES)]
-
-        def passes_b(unit):
-            count = 0
-            for g, i in list(open_passes):
-                ready = max(done.get((g, 128 * i), 99), ASTART[i])
-                if count < CAP and ready + LAG <= unit and all((q, i) not in open_passes for q in range(g)):
-                    stage2(g, (i,))
-                    open_passes.remove((g, i))
-                    count += 1
-
-        for unit, (half, g, n0, width) in enumerate(units):
-
-            def passes():
-                if unit in pass_step:
-                    stage2(pass_step[unit], range(4))
-                if half == 1:
-                    passes_b(unit)
-
-            if width == 512:
-                stage1(half, g, passes)
+        for g in range(GROUPS):
+            first_layer(0, g)
+            if g >= 2:
+                second_layer(0, g - 2, 0)
+                second_layer(0, g - 2, 1)
+            if g + 2 < GROUPS:
+                turn_w1(g + 2)
+            if g == 0:
+                normalise_x(1, 0)
+                normalise_x(1, 1)
+                interleave_x(1, 0)
+                interleave_x(1, 1)
+                quantize(x_codes[1], x_slots[1])
             else:
-                stage1_quarter(half, g, n0 // 256, passes)
-            if unit + 2 < GROUPS:
-                prep_w1(unit + 2)
-            if unit in w2_step:
-                prep_w2(w2_step[unit])
-            if unit == XB:
-                x_inter[0] = x_path(1, XBV)
-            count = PCNT.get(unit, 0)
-            for item in VORD:
-                if item == "e":
-                    epilogue(unit)
-                if item == "p":
-                    scale_next((count + 1) // 2)
-                if item == "q":
-                    scale_next(count // 2)
-                if item == "i":
-                    inter_h(g, width)
-                if item == "1" and unit + 2 < GROUPS:
-                    quantize(w1c[unit + 2], w1g[unit + 2])
-                if item == "h":
-                    quant_h(g, n0, width)
-                    if half == 1:
-                        for q in range(n0, n0 + width, 128):
-                            done[g, q] = unit
-                if item == "x" and unit == XB:
-                    quantize(xc[1], x_inter[0])
-                if item == "2" and unit in w2_step:
-                    quantize(w2c[w2_step[unit]], w2g[w2_step[unit]])
+                first_layer(1, g - 1)
+            if g >= 2:
+                second_layer(0, g - 2, 2)
+                second_layer(0, g - 2, 3)
+            turn_w2(g)
+            if g == 3:
+                load_epilogue_rows()
+            interleave_h(0, g)
+            if g + 2 < GROUPS:
+                quantize(w1_codes[g + 2], w1_slots[g + 2])
+            if g < 5:
+                scale_w2_row()
+            if g > 0:
+                interleave_h(1, g - 1)
+            quantize(h_codes[0][g], h_slots[0, g])
+            if g < 5:
+                scale_w2_row()
+            quantize(w2_codes[g], w2_slots[g])
+            if g > 0:
+                quantize(h_codes[1][g - 1], h_slots[1, g - 1])
 
-        for g, i in list(open_passes):
-            stage2(g, (i,))
-        last = len(units)
-        assert max(ASTART) + 3 < last and all(BSTART[i] > ASTART[i] + 3 for i in range(2))
-        for stage in range(4):
-            for i in range(TILES):
-                start = BSTART[i] if i < 2 else last
-                if start + stage >= last:
-                    epilogue_stage(1, i, stage)
+        last = GROUPS - 1
+        for item in LAST_STRETCH.split():
+            if item == "h":
+                first_layer(1, last)
+            elif item == "i":
+                interleave_h(1, last)
+            elif item == "k":
+                quantize(h_codes[1][last], h_slots[1, last])
+            elif item == "a":
+                for g in (last - 1, last):
+                    for i in range(TILES):
+                        second_layer(0, g, i)
+            else:
+                half, i = int(item[1]) // TILES, int(item[1]) % TILES
+                if item[0] == "b":
+                    for g in range(last):
+                        second_layer(1, g, i)
+                elif item[0] == "z":
+                    second_layer(1, last, i)
+                elif item[0] == "r":
+                    add_bias(half, i)
+                elif item[0] == "s":
+                    scale_out(half, i)
+                elif item[0] == "m":
+                    add_residual(half, i)
+                else:
+                    divide_and_store(half, i)

from contextlib import ExitStack

import concourse.mybir as mybir
from concourse.masks import make_identity

B, D_IN, D_HID, D_OUT = 1024, 512, 4096, 512
FLOPS = 2 * B * D_IN * D_HID + 2 * B * D_HID * D_OUT

F32 = mybir.dt.float32
BF16 = mybir.dt.bfloat16
U32 = mybir.dt.uint32
U8 = mybir.dt.uint8
FP8 = mybir.dt.float8_e4m3fn
FP8X4 = mybir.dt.float8_e4m3fn_x4
OP = mybir.AluOpType
ACT = mybir.ActivationFunctionType

P = 128
GROUP = 512
GROUPS = D_HID // GROUP
HALF = B // 2
TILES = HALF // P
CHUNK = 2 * GROUP
EPS_SQUARED = 1e-24

LAST_STRETCH = (
    "h a r0 r1 b4 r2 i r3 s0 k s2 b5 m0 z4 s1 z5 m1 r4 m2 o1 b7 s3 r5 o0 s4 o2 m3 s5 m4 b6 z6 z7 r6 r7 m5 o4 s6 o3 "
    "s7 m6 m7 o5 o6 o7"
)


def tile_mlp_kernel(
    tc, x, in_mean, in_std, out_mean, out_std, W1, b1, W2_bytes, W2_scale, b2, norm_max, out
):
    nc = tc.nc
    inverse_square_of_norm_max = 1.0 / (float(norm_max) * float(norm_max))

    with ExitStack() as ctx:
        keep = ctx.enter_context(tc.tile_pool(name="keep", bufs=1))
        pool = ctx.enter_context(tc.tile_pool(name="work", bufs=2))
        psum = ctx.enter_context(tc.psum_pool(name="psum", bufs=1))
        ctx.enter_context(tc.manual_schedule())

        def kept(name, shape, dtype):
            return keep.tile(shape, dtype, name=name, align_bytes=64)

        def work(tag, shape, dtype, bufs):
            return pool.tile(shape, dtype, name=tag, tag=tag, bufs=bufs, align_bytes=64)

        banks_used = [0]

        def next_bank():
            tag = "ring%d" % (banks_used[0] % 4)
            banks_used[0] += 1
            return psum.tile([P, 512], F32, name=tag, tag=tag)

        in_mean_columns = kept("in_mean_columns", [P, 4], BF16)
        in_std_columns = kept("in_std_columns", [P, 4], BF16)
        b1_rows = kept("b1_rows", [P, 512], BF16)
        mean_rows = kept("mean_rows", [P, 512], BF16)
        b2_everywhere = kept("b2_everywhere", [P, D_OUT], BF16)
        out_std_everywhere = kept("out_std_everywhere", [P, D_OUT], BF16)
        x_rows = {}
        for half in range(2):
            for pair in range(2):
                x_rows[half, pair] = kept("x_rows%d%d" % (half, pair), [P, 2, D_IN], BF16)
        w1_rows, w2_bytes, w2_scales = {}, {}, {}

        def load_x(half):
            rows = x[half * HALF : (half + 1) * HALF, :].rearrange("(q i) k -> q i k", i=TILES)
            for pair in range(2):
                nc.sync.dma_start(out=x_rows[half, pair][:], in_=rows[:, 2 * pair : 2 * pair + 2, :])

        def load_w1(g):
            w1_rows[g] = work("w1_rows", [P, 4, D_IN], BF16, 4)
            nc.sync.dma_start(
                out=w1_rows[g][:], in_=W1[GROUP * g : GROUP * (g + 1), :].rearrange("(m t) k -> m t k", t=4)
            )

        def load_w2_scales(c):
            w2_scales[c] = work("w2_scales", [P, CHUNK], F32, 2)
            row = W2_scale[:, CHUNK * c : CHUNK * (c + 1)].rearrange("o k -> (o k)")
            nc.sync.dma_start(out=w2_scales[c][:], in_=row.partition_broadcast(P))

        def load_w2_bytes(c):
            w2_bytes[c] = work("w2_bytes", [P, 4, CHUNK], U8, 2)
            columns = W2_bytes[:, CHUNK * c : CHUNK * (c + 1)]
            nc.sync.dma_start(out=w2_bytes[c][:], in_=columns.rearrange("(j q) k -> q j k", q=P))

        nc.vector.memset(b1_rows[:], 0.0)
        nc.gpsimd.memset(mean_rows[:], 0.0)
        scratch = kept("scratch", [P, 1], F32)
        nc.vector.memset(scratch[:], 0.0)

        load_x(0)
        nc.sync.dma_start(out=in_mean_columns[:], in_=in_mean.rearrange("(p t) -> p t", t=4))
        nc.sync.dma_start(out=in_std_columns[:], in_=in_std.rearrange("(p t) -> p t", t=4))
        load_w1(0)
        nc.sync.dma_start(out=b1_rows[0:GROUPS, :], in_=b1.rearrange("(g k) -> g k", g=GROUPS))
        load_w2_bytes(0)
        load_w2_scales(0)
        load_w1(1)
        load_x(1)
        load_w1(2)
        load_w2_bytes(1)
        load_w2_scales(1)
        load_w1(3)

        def load_epilogue_rows():
            nc.sync.dma_start(out=mean_rows[0:1, :], in_=out_mean.rearrange("(o k) -> o k", o=1))
            nc.sync.dma_start(out=mean_rows[1:2, :], in_=in_mean.rearrange("(o k) -> o k", o=1))
            nc.sync.dma_start(out=b2_everywhere[:], in_=b2.partition_broadcast(P))
            nc.sync.dma_start(out=out_std_everywhere[:], in_=out_std.partition_broadcast(P))

        identity = kept("identity", [P, P], F32)
        make_identity(nc, identity[:])
        identity_bf16 = kept("identity_bf16", [P, P], BF16)
        make_identity(nc, identity_bf16[:])
        minus_half = kept("minus_half", [P, 1], F32)
        nc.gpsimd.memset(minus_half[:], -0.5)
        nc.scalar.activation(out=scratch[:], in_=scratch[:], func=ACT.Relu)

        def codes(name):
            return kept(name + "_codes", [P, 512], U32), kept(name + "_scales", [P, 512], U8)

        x_codes = [codes("x%d" % half) for half in range(2)]
        w1_codes = [codes("w1_%d" % g) for g in range(GROUPS)]
        w2_codes = [codes("w2_%d" % g) for g in range(GROUPS)]
        h_codes = [[codes("h%d_%d" % (half, g)) for g in range(GROUPS)] for half in range(2)]

        def quantize(operand, slots):
            nc.vector.quantize_mx(
                out=operand[0][:].bitcast(FP8X4), scales=operand[1][:], in_=slots[:].rearrange("p n t -> p (n t)")
            )

        def interleave(slots, planes):
            nc.vector.tensor_copy(
                out=slots.rearrange("p (c i) t -> p c t i", i=4), in_=planes.rearrange("p t (c i) -> p c t i", i=4)
            )

        in_rstd = kept("in_rstd", [P, 4], F32)
        in_mean_f32 = kept("in_mean_f32", [P, 4], F32)
        in_shift = kept("in_shift", [P, 4], F32)
        nc.vector.reciprocal(out=in_rstd[:], in_=in_std_columns[:])
        nc.vector.tensor_copy(out=in_mean_f32[:], in_=in_mean_columns[:])
        nc.vector.scalar_tensor_tensor(
            out=in_shift[:], in0=in_mean_columns[:], scalar=-1.0, in1=in_rstd[:], op0=OP.mult, op1=OP.mult
        )
        mean_picker = kept("mean_picker", [P, 1], BF16)
        nc.vector.tensor_sub(out=mean_picker[:], in0=identity_bf16[:, 0:1], in1=identity_bf16[:, 1:2])

        x_planes, x_slots = {}, {}

        def normalise_x(half, pair):
            if pair == 0:
                x_planes[half] = work("planes", [P, 4, 512], BF16, 3)
                x_slots[half] = work("slots", [P, 512, 4], BF16, 3)
            bank = next_bank()
            words = x_rows[half, pair][:].bitcast(F32)
            for u in range(2):
                for i in range(2):
                    first = 256 * u + 128 * i
                    nc.tensor.transpose(bank[:, first : first + 128], words[:, i, u:256:2], identity[:])
            tokens = slice(256 * pair, 256 * pair + 256)
            for t in range(4):
                u, e = t // 2, t % 2
                both = bank[:, 256 * u : 256 * u + 256].bitcast(BF16).rearrange("p (n e) -> p e n", e=2)
                if pair == 1:
                    nc.vector.tensor_scalar(
                        out=x_planes[half][:, t, tokens],
                        in0=both[:, e, :],
                        scalar1=in_mean_f32[:, t : t + 1],
                        scalar2=in_rstd[:, t : t + 1],
                        op0=OP.subtract,
                        op1=OP.mult,
                    )
                else:
                    nc.scalar.activation(
                        out=x_planes[half][:, t, tokens],
                        in_=both[:, e, :],
                        func=ACT.Identity,
                        scale=in_rstd[:, t : t + 1],
                        bias=in_shift[:, t : t + 1],
                    )

        def interleave_x(half, pair):
            tokens = slice(256 * pair, 256 * pair + 256)
            interleave(x_slots[half][:, tokens, :], x_planes[half][:, :, tokens])

        w1_slots, w2_scaled, w2_slots = {}, {}, {}

        def turn(slots, words, first):
            bank = next_bank()
            for s in range(2):
                for u in range(2):
                    column = 256 * s + 128 * u
                    nc.tensor.transpose(bank[:, column : column + 128], words[:, first + s, u:256:2], identity[:])
            nc.scalar.copy(
                out=slots[:].bitcast(F32)[:, 128 * first : 128 * first + 256, :].rearrange("p (s m) u -> p s m u", s=2),
                in_=bank[:].rearrange("p (s u m) -> p s m u", s=2, u=2),
            )

        def turn_w1(g):
            w1_slots[g] = work("w1_slots", [P, 512, 4], BF16, 2)
            for first in (0, 2):
                turn(w1_slots[g], w1_rows[g][:].bitcast(F32), first)
            if g + 4 < GROUPS:
                load_w1(g + 4)

        scaled_rows = [0]

        def scale_w2_row():
            c, j = scaled_rows[0] // 4, scaled_rows[0] % 4
            if j == 0:
                w2_scaled[c] = work("w2_scaled", [P, 4, CHUNK], BF16, 2)
            nc.vector.tensor_tensor(
                out=w2_scaled[c][:, j, :], in0=w2_bytes[c][:, j, :].bitcast(FP8), in1=w2_scales[c][:], op=OP.mult
            )
            scaled_rows[0] += 1
            if j == 3 and c + 2 < D_HID // CHUNK:
                load_w2_scales(c + 2)
                load_w2_bytes(c + 2)

        def turn_w2(g):
            w2_slots[g] = work("w2_slots", [P, 512, 4], BF16, 2)
            words = w2_scaled[g // 2][:].bitcast(F32)[:, :, 256 * (g % 2) : 256 * (g % 2) + 256]
            for first in (0, 2):
                turn(w2_slots[g], words, first)

        b1_words = kept("b1_words", [P, GROUPS, 2], F32)
        b1_columns = kept("b1_columns", [P, 4 * GROUPS], F32)

        def turn_b1():
            bank = next_bank()
            words = b1_rows[:].bitcast(F32)
            for u in range(2):
                nc.tensor.transpose(bank[:, 128 * u : 128 * u + 128], words[:, u:256:2], identity[:])
            nc.vector.tensor_copy(
                out=b1_words[:], in_=bank[:, 0:256].rearrange("p (u g) -> p g u", u=2)[:, 0:GROUPS, :]
            )
            nc.vector.tensor_copy(out=b1_columns[:], in_=b1_words[:].rearrange("p g u -> p (g u)").bitcast(BF16))

        h_planes, h_slots = {}, {}

        def first_layer(half, g):
            h_planes[half, g] = work("planes", [P, 4, 512], BF16, 3)
            for t in range(4):
                bank = next_bank()
                channels = slice(128 * t, 128 * t + 128)
                nc.tensor.matmul_mx(
                    out=bank[:],
                    lhsT=w1_codes[g][0][:, channels].bitcast(FP8X4),
                    lhsT_scale=w1_codes[g][1][:, channels],
                    rhs=x_codes[half][0][:].bitcast(FP8X4),
                    rhs_scale=x_codes[half][1][:],
                    start=True,
                    stop=True,
                )
                nc.scalar.activation(
                    out=h_planes[half, g][:, t, :],
                    in_=bank[:],
                    func=ACT.Relu,
                    bias=b1_columns[:, 4 * g + t : 4 * g + t + 1],
                )

        def interleave_h(half, g):
            h_slots[half, g] = work("slots", [P, 512, 4], BF16, 3)
            interleave(h_slots[half, g][:], h_planes[half, g][:])

        sums = {}

        def second_layer(half, g, i):
            if g == 0:
                sums[i] = psum.tile([P, 512], F32, name="sums%d" % i, tag="sums%d" % i)
            tokens = slice(128 * i, 128 * i + 128)
            nc.tensor.matmul_mx(
                out=sums[i][:],
                lhsT=h_codes[half][g][0][:, tokens].bitcast(FP8X4),
                lhsT_scale=h_codes[half][g][1][:, tokens],
                rhs=w2_codes[g][0][:].bitcast(FP8X4),
                rhs_scale=w2_codes[g][1][:],
                start=(g == 0),
                stop=(g == GROUPS - 1),
            )

        res, scaled, mapped, res_squares, clamp, mapped_squares, reciprocal_norm = {}, {}, {}, {}, {}, {}, {}

        def row_squares(tile, name):
            squares = work("squares", [P, 512], BF16, 2)
            total = work(name, [P, 1], F32, 4)
            nc.scalar.activation(out=squares[:], in_=tile[:], func=ACT.Square, accum_out=total[:])
            return total

        def add_bias(half, i):
            res[half, i] = work("res", [P, 512], F32, 4)
            nc.vector.tensor_add(out=res[half, i][:], in0=sums[i][:], in1=b2_everywhere[:])
            res_squares[half, i] = row_squares(res[half, i], "res_squares")

        def scale_out(half, i):
            scaled[half, i] = work("scaled", [P, 512], F32, 4)
            nc.vector.tensor_mul(out=scaled[half, i][:], in0=res[half, i][:], in1=out_std_everywhere[:])
            ratio = work("ratio", [P, 1], F32, 4)
            clamp[half, i] = work("clamp", [P, 1], F32, 4)
            nc.gpsimd.tensor_scalar(
                out=ratio[:],
                in0=res_squares[half, i][:],
                scalar1=inverse_square_of_norm_max,
                scalar2=1.0,
                op0=OP.mult,
                op1=OP.max,
            )
            nc.gpsimd.tensor_tensor(out=clamp[half, i][:], in0=ratio[:], in1=minus_half[:], op=OP.pow)

        def add_residual(half, i):
            bank = next_bank()
            nc.tensor.matmul(
                out=bank[:], lhsT=identity_bf16[:], rhs=x_rows[half, i // 2][:, i % 2, :], start=True, stop=False
            )
            nc.tensor.matmul(
                out=bank[:], lhsT=mean_picker[:, 0:1].to_broadcast([P, P]), rhs=mean_rows[:], start=False, stop=True
            )
            mapped[half, i] = work("mapped", [P, 512], F32, 4)
            nc.vector.scalar_tensor_tensor(
                out=mapped[half, i][:],
                in0=scaled[half, i][:],
                scalar=clamp[half, i][:, 0:1],
                in1=bank[:],
                op0=OP.mult,
                op1=OP.add,
            )
            mapped_squares[half, i] = row_squares(mapped[half, i], "mapped_squares")

        def divide_and_store(half, i):
            floored = work("floored", [P, 1], F32, 4)
            reciprocal_norm[half, i] = work("reciprocal_norm", [P, 1], F32, 4)
            nc.gpsimd.tensor_scalar(
                out=floored[:],
                in0=mapped_squares[half, i][:],
                scalar1=EPS_SQUARED,
                scalar2=0.0,
                op0=OP.max,
                op1=OP.add,
            )
            nc.gpsimd.tensor_tensor(out=reciprocal_norm[half, i][:], in0=floored[:], in1=minus_half[:], op=OP.pow)
            final = work("final", [P, 512], F32, 3)
            if half == 1:
                nc.vector.tensor_scalar_mul(
                    out=final[:], in0=mapped[half, i][:], scalar1=reciprocal_norm[half, i][:, 0:1]
                )
            else:
                nc.scalar.activation(
                    out=final[:], in_=mapped[half, i][:], func=ACT.Copy, scale=reciprocal_norm[half, i][:, 0:1]
                )
            rows = out[half * HALF : (half + 1) * HALF, :].rearrange("(q i) n -> q i n", i=TILES)
            nc.sync.dma_start(out=rows[:, i, :], in_=final[:])

        normalise_x(0, 0)
        normalise_x(0, 1)
        turn_w1(0)
        interleave_x(0, 1)
        turn_b1()
        interleave_x(0, 0)
        quantize(x_codes[0], x_slots[0])
        quantize(w1_codes[0], w1_slots[0])
        scale_w2_row()
        scale_w2_row()
        scale_w2_row()
        turn_w1(1)
        scale_w2_row()
        quantize(w1_codes[1], w1_slots[1])
        scale_w2_row()
        scale_w2_row()

        for g in range(GROUPS):
            first_layer(0, g)
            if g >= 2:
                second_layer(0, g - 2, 0)
                second_layer(0, g - 2, 1)
            if g + 2 < GROUPS:
                turn_w1(g + 2)
            if g == 0:
                normalise_x(1, 0)
                normalise_x(1, 1)
                interleave_x(1, 0)
                interleave_x(1, 1)
                quantize(x_codes[1], x_slots[1])
            else:
                first_layer(1, g - 1)
            if g >= 2:
                second_layer(0, g - 2, 2)
                second_layer(0, g - 2, 3)
            turn_w2(g)
            if g == 3:
                load_epilogue_rows()
            interleave_h(0, g)
            if g + 2 < GROUPS:
                quantize(w1_codes[g + 2], w1_slots[g + 2])
            if g < 5:
                scale_w2_row()
            if g > 0:
                interleave_h(1, g - 1)
            quantize(h_codes[0][g], h_slots[0, g])
            if g < 5:
                scale_w2_row()
            quantize(w2_codes[g], w2_slots[g])
            if g > 0:
                quantize(h_codes[1][g - 1], h_slots[1, g - 1])

        last = GROUPS - 1
        for item in LAST_STRETCH.split():
            if item == "h":
                first_layer(1, last)
            elif item == "i":
                interleave_h(1, last)
            elif item == "k":
                quantize(h_codes[1][last], h_slots[1, last])
            elif item == "a":
                for g in (last - 1, last):
                    for i in range(TILES):
                        second_layer(0, g, i)
            else:
                half, i = int(item[1]) // TILES, int(item[1]) % TILES
                if item[0] == "b":
                    for g in range(last):
                        second_layer(1, g, i)
                elif item[0] == "z":
                    second_layer(1, last, i)
                elif item[0] == "r":
                    add_bias(half, i)
                elif item[0] == "s":
                    scale_out(half, i)
                elif item[0] == "m":
                    add_residual(half, i)
                else:
                    divide_and_store(half, i)
